import numpy as np
import ml_dtypes


def mxq(x, axis, fmt="e4m3"):
    dtype, down = {"e4m3": (ml_dtypes.float8_e4m3fn, 7), "e5m2": (ml_dtypes.float8_e5m2, 14)}[fmt]
    v = np.moveaxis(np.asarray(x, np.float32).astype(ml_dtypes.bfloat16).astype(np.float64), axis, -1)
    blocks = v.reshape(v.shape[:-1] + (-1, 32))
    amax = np.abs(blocks).max(-1, keepdims=True)
    byte = np.maximum(np.where(amax > 0, np.frexp(amax)[1] - 1 + 127, 0) - down, 1)
    scale = np.exp2(byte - 127.0)
    codes = (blocks / scale).astype(np.float32).astype(dtype).astype(np.float64)
    return np.moveaxis((codes * scale).reshape(v.shape), -1, axis)


WIDE = False


def mx_kscale(k):
    if not WIDE:
        return np.ones(k)
    levels = np.array([18, -18])
    if k % 512:
        return np.exp2(np.random.permutation(np.resize(levels, k // 32))).repeat(32)
    a = np.empty((k // 512, 16))
    for p in range(k // 512):
        a[p, :8] = np.random.permutation(np.resize(levels, 8))
        for g in range(8):
            far = levels[np.abs(levels - a[p, g]) >= 10]
            a[p, g + 8] = far[np.random.randint(len(far))]
    return np.exp2(a.ravel()).repeat(32)


BF16 = ml_dtypes.bfloat16


def bf(x):
    return np.asarray(x, np.float32).astype(BF16)


def f64(x):
    return np.asarray(x).astype(np.float64)


B, I, H = 512, 1024, 1024


def sigmoid(v):
    return 1.0 / (1.0 + np.exp(-v))


def setup_inputs():
    s = mx_kscale(B)[:, None]
    u = mx_kscale(H)
    d = {"x_t": bf(np.random.standard_normal((B, I))),
         "h_prev": bf(np.random.standard_normal((B, H))),
         "c_prev": bf(np.random.standard_normal((B, H)))}
    for k in ("f", "i", "c", "o"):
        d["W_" + k] = bf(np.random.standard_normal((I, H)) * 0.7 / np.sqrt(I))
    for k in ("f", "i", "c", "o"):
        d["U_" + k] = bf(np.random.standard_normal((H, H)) * 0.7 / np.sqrt(H))
    for k in ("f", "i", "c", "o"):
        d["b_" + k] = bf(np.random.standard_normal(H) * 0.1)
    gates = np.concatenate(
        [f64(d["x_t"]) @ f64(d["W_" + k]) + f64(d["h_prev"]) @ f64(d["U_" + k]) + f64(d["b_" + k])
         for k in ("f", "i", "c", "o")], axis=1)
    d["x_t"] = bf(f64(d["x_t"]) * s)
    for k in ("f", "i", "c", "o"):
        d["W_" + k] = bf(f64(d["W_" + k]) / u)
    d["gates"] = np.asarray(gates, np.float32)
    d["grad_out"] = bf(np.random.standard_normal((B, H)) * np.exp2(np.random.randint(-6, 1, (B, 1))) * 16.0 / s * u)
    return d


def reference(x_t, h_prev, c_prev, W_f, W_i, W_c, W_o, U_f, U_i, U_c, U_o, b_f, b_i, b_c, b_o, gates, grad_out):
    a = f64(gates)
    g = f64(grad_out)
    cp = f64(c_prev)
    f_t = sigmoid(a[:, 0 * H:1 * H])
    i_t = sigmoid(a[:, 1 * H:2 * H])
    c_tilda_t = np.tanh(a[:, 2 * H:3 * H])
    o_t = sigmoid(a[:, 3 * H:4 * H])
    tc = np.tanh(f_t * cp + i_t * c_tilda_t)
    dc = g * o_t * (1.0 - tc * tc)
    dz_f = dc * cp * f_t * (1.0 - f_t)
    dz_i = dc * c_tilda_t * i_t * (1.0 - i_t)
    dz_c = dc * i_t * (1.0 - c_tilda_t * c_tilda_t)
    dz_o = g * tc * o_t * (1.0 - o_t)
    dz = np.concatenate([dz_f, dz_i, dz_c, dz_o], axis=1)
    W = np.concatenate([f64(W_f), f64(W_i), f64(W_c), f64(W_o)], axis=1)
    dx = mxq(dz, 1, "e5m2") @ mxq(W, 1, "e4m3").T
    dw = mxq(f64(x_t), 0, "e4m3").T @ mxq(dz_f, 0, "e5m2")
    return dx, dw

@@ -1,0 +1,403 @@
+from contextlib import ExitStack
+
+import concourse.mybir as mybir
+from concourse.masks import make_identity
+
+B, I, H = 512, 1024, 1024
+FLOPS = 2 * B * 4 * H * I + 2 * I * B * H
+BYTES = (B * I + 2 * B * H + 4 * I * H) * 2 + (B * 4 * H + B * I + I * H) * 4
+
+F32 = mybir.dt.float32
+BF16 = mybir.dt.bfloat16
+U32 = mybir.dt.uint32
+U8 = mybir.dt.uint8
+E4M3 = mybir.dt.float8_e4m3fn_x4
+E5M2 = mybir.dt.float8_e5m2_x4
+ACT = mybir.ActivationFunctionType
+ALU = mybir.AluOpType
+
+P = 128
+PACK = 4
+K_PASS = P * PACK
+GATES = 4
+HALVES = 2
+TILES = HALVES * PACK
+ORDER = ((0, 0), (0, 1), (1, 0), (1, 1), (2, 0), (3, 0), (2, 1), (3, 1))
+
+
+def tile_lstmcell_v_kernel(
+    tc, x_t, h_prev, c_prev, W_f, W_i, W_c, W_o, U_f, U_i, U_c, U_o, b_f, b_i, b_c, b_o, gates, grad_out, out_0, out_1
+):
+    nc = tc.nc
+    weights = (W_f, W_i, W_c, W_o)
+    gates_v = gates.rearrange("(p j) (k h) -> p j k h", j=PACK, k=GATES)
+    cprev_v = c_prev.rearrange("(p j) h -> p j h", j=PACK)
+    grad_v = grad_out.rearrange("(p j) h -> p j h", j=PACK)
+    x_v = x_t.rearrange("(p j) i -> p j i", j=PACK)
+    out0_v = out_0.rearrange("(p j) i -> p j i", j=PACK)
+
+    with ExitStack() as ctx:
+        sb = ctx.enter_context(tc.tile_pool(name="sb", bufs=1))
+        ps = ctx.enter_context(tc.psum_pool(name="ps", bufs=1))
+        ctx.enter_context(tc.manual_schedule())
+
+        ident = sb.tile([P, P], F32, name="ident")
+        make_identity(nc, ident[:])
+
+        raw_gates, raw_cp, raw_g, raw_w, raw_x = {}, {}, {}, {}, {}
+        sig, ct, ct2, prod, neg_p, ndc, ntc, tc2 = {}, {}, {}, {}, {}, {}, {}, {}
+        banks, dz_t, dz_q, w_q, x_q, dzf_q, grouped, accs = {}, {}, {}, {}, {}, {}, {}, {}
+
+        def cols(g):
+            return slice(g * K_PASS, (g + 1) * K_PASS)
+
+        def blk(t):
+            return slice(t * P, (t + 1) * P)
+
+        def load_gates(s):
+            j, g = ORDER[s]
+            raw_gates[s] = []
+            for half in range(2):
+                t = sb.tile([P, 2 * K_PASS], F32, name="raw_gates", bufs=6)
+                raw_gates[s].append(t)
+                nc.sync.dma_start(
+                    out=t[:].rearrange("p (k h) -> p k h", k=2), in_=gates_v[:, j, 2 * half : 2 * half + 2, cols(g)]
+                )
+                if g == 0:
+                    name, src, dst = (("raw_cp", cprev_v, raw_cp), ("raw_g", grad_v, raw_g))[half]
+                    dst[j] = sb.tile([P, H], BF16, name=name, bufs=3)
+                    nc.sync.dma_start(out=dst[j][:], in_=src[:, j, :])
+
+        def load_w(u):
+            n, k = divmod(u, GATES)
+            raw_w[u] = sb.tile([P, PACK, H], BF16, name="raw_w", bufs=3)
+            nc.sync.dma_start(out=raw_w[u][:], in_=weights[k][cols(n), :].rearrange("(b p) h -> p b h", p=P))
+
+        def load_x(n):
+            raw_x[n] = sb.tile([P, PACK, K_PASS], BF16, name="raw_x", bufs=1)
+            nc.sync.dma_start(out=raw_x[n][:], in_=x_v[:, :, cols(n)])
+
+        def new_grouped(key):
+            grouped[key] = sb.tile([P, PACK * K_PASS], BF16, name="grouped", bufs=6, align_bytes=64)
+            return grouped[key]
+
+        def quantize(src, fmt, name, bufs):
+            codes = sb.tile([P, K_PASS], U32, name=name + "_codes", bufs=bufs, align_bytes=64)
+            scales = sb.tile([P, K_PASS], U8, name=name + "_scales", bufs=bufs, align_bytes=64)
+            nc.vector.quantize_mx(out=codes[:].bitcast(fmt), scales=scales[:], in_=src[:])
+            return codes, scales
+
+        def interleave_x(n, copy):
+            dst = new_grouped(("x", n))
+            copy(
+                out=dst[:].rearrange("p (c i t) -> p c t i", i=4, t=PACK),
+                in_=raw_x[n][:].rearrange("p t (c i) -> p c t i", i=4),
+            )
+
+        def quantize_x(n):
+            x_q[n] = quantize(grouped[("x", n)], E4M3, "x", 2)
+
+        def sorted_in(ap):
+            return ap.rearrange("p (a i t) -> p a t i", i=2, t=PACK)
+
+        def sorted_out(ap):
+            return ap.rearrange("p t (a i) -> p a t i", i=2)
+
+        def activations(s):
+            fi, co = raw_gates[s]
+            sig[s] = sb.tile([P, PACK, 3 * P], F32, name="sig", bufs=2)
+            ct[s] = sb.tile([P, PACK, P], F32, name="ct", bufs=2)
+            ct2[s] = sb.tile([P, PACK, P], F32, name="ct2", bufs=2)
+            nc.scalar.activation(out=sorted_out(sig[s][:, :, 0 : 2 * P]), in_=sorted_in(fi[:]), func=ACT.Sigmoid)
+            nc.scalar.activation(out=sorted_out(ct[s][:]), in_=sorted_in(co[:, 0:K_PASS]), func=ACT.Tanh)
+            nc.scalar.activation(out=sorted_out(sig[s][:, :, blk(2)]), in_=sorted_in(co[:, K_PASS:]), func=ACT.Sigmoid)
+            nc.scalar.activation(out=ct2[s][:], in_=ct[s][:], func=ACT.Square)
+
+        def products(s):
+            prod[s] = sb.tile([P, PACK, 3 * P], F32, name="prod", bufs=2)
+            j, g = ORDER[s]
+            cp = raw_cp[j][:, cols(g)].rearrange("p (m t) -> p t m", t=PACK)
+            gr = raw_g[j][:, cols(g)].rearrange("p (m t) -> p t m", t=PACK)
+            nc.vector.tensor_tensor(out=prod[s][:, :, blk(0)], in0=sig[s][:, :, blk(0)], in1=cp, op=ALU.mult)
+            nc.vector.tensor_tensor(out=prod[s][:, :, blk(1)], in0=sig[s][:, :, blk(1)], in1=ct[s][:], op=ALU.mult)
+            nc.vector.tensor_tensor(out=prod[s][:, :, blk(2)], in0=sig[s][:, :, blk(2)], in1=gr, op=ALU.mult)
+
+        def factor(s, key, out, in0, in1):
+            neg_p[s, key] = out
+            nc.vector.scalar_tensor_tensor(out=out, in0=in0, scalar=1.0, in1=in1, op0=ALU.subtract, op1=ALU.mult)
+
+        def factor_f(s):
+            t = sb.tile([P, PACK, P], F32, name="neg_pf", bufs=1)
+            factor(s, "f", t[:], sig[s][:, :, blk(0)], prod[s][:, :, blk(0)])
+
+        def factor_io(s):
+            t = sb.tile([P, PACK, 2 * P], F32, name="neg_pio", bufs=1)
+            factor(s, "io", t[:], sig[s][:, :, P:], prod[s][:, :, P:])
+            neg_p[s, "i"], neg_p[s, "o"] = t[:, :, blk(0)], t[:, :, blk(1)]
+
+        def factor_c(s):
+            t = sb.tile([P, PACK, P], F32, name="neg_pc", bufs=1)
+            factor(s, "cc", t[:], ct2[s][:], sig[s][:, :, blk(1)])
+
+        free_banks = list(range(8))
+        bank_of = {}
+
+        def take_bank(key):
+            bank_of[key] = free_banks.pop(0)
+            banks[key] = ps.tile([P, K_PASS], F32, name="bank%d" % bank_of[key])
+            return banks[key]
+
+        def give_bank(key):
+            free_banks.append(bank_of[key])
+
+        def transpose_cell(s):
+            bank = take_bank((s, "c"))
+            for t in range(PACK):
+                for term in range(2):
+                    nc.tensor.matmul(
+                        out=bank[:, blk(t)], lhsT=prod[s][:, t, blk(term)], rhs=ident[:],
+                        is_transpose=True, start=(term == 0), stop=(term == 1),
+                    )
+
+        def transpose_factors(s, keys):
+            for key in keys:
+                src = prod[s][:, :, blk(2)] if key == "go" else neg_p[s, key]
+                bank = take_bank((s, key))
+                for t in range(PACK):
+                    nc.tensor.transpose(bank[:, blk(t)], src[:, t, :], ident[:])
+
+        def packed(s, key):
+            return banks[s, key][:].rearrange("p (t n) -> p n t", t=PACK)
+
+        def cell_tanh(s):
+            ntc[s] = sb.tile([P, P, PACK], F32, name="ntc", bufs=2)
+            tc2[s] = sb.tile([P, P, PACK], F32, name="tc2", bufs=1)
+            nc.scalar.activation(out=ntc[s][:], in_=packed(s, "c"), func=ACT.Tanh, scale=-1.0)
+            give_bank((s, "c"))
+            nc.scalar.activation(out=tc2[s][:], in_=ntc[s][:], func=ACT.Square)
+
+        def grad_cell(s):
+            ndc[s] = sb.tile([P, P, PACK], F32, name="ndc", bufs=2)
+            nc.vector.scalar_tensor_tensor(
+                out=ndc[s][:], in0=tc2[s][:], scalar=1.0, in1=packed(s, "go"), op0=ALU.subtract, op1=ALU.mult
+            )
+            give_bank((s, "go"))
+
+        def grad_gate(s, key):
+            if key == "f":
+                dz_t[s, "f"] = sb.tile([P, K_PASS], BF16, name="dz_f", bufs=TILES, align_bytes=64)[:]
+            if key == "o":
+                t = sb.tile([P, 3 * K_PASS], BF16, name="dz_oic", bufs=2, align_bytes=64)
+                dz_t[s, "o"], dz_t[s, "i"], dz_t[s, "cc"] = t[:, cols(0)], t[:, cols(1)], t[:, cols(2)]
+                dz_t[s, "oi"] = t[:, 0 : 2 * K_PASS]
+            nc.vector.tensor_tensor(
+                out=dz_t[s, key].rearrange("p (n t) -> p n t", t=PACK),
+                in0=(ntc if key == "o" else ndc)[s][:], in1=packed(s, key), op=ALU.mult,
+            )
+            give_bank((s, key))
+
+        def quantize_dz(s, key):
+            if key == "f":
+                codes = sb.tile([P, K_PASS], U32, name="dz_codes", bufs=6, align_bytes=64)
+                scales = sb.tile([P, K_PASS], U8, name="dz_scales", bufs=6, align_bytes=64)
+                dz_q[ORDER[s]] = codes, scales
+            codes, scales = dz_q[ORDER[s]]
+            span = {"f": blk(0), "oi": slice(P, 3 * P), "o": blk(1), "i": blk(2), "cc": blk(3)}[key]
+            nc.vector.quantize_mx(out=codes[:, span].bitcast(E5M2), scales=scales[:, span], in_=dz_t[s, key])
+
+        def turn_w(u):
+            words = raw_w[u][:].bitcast(F32)
+            for g in range(HALVES):
+                dst = new_grouped(("w", u, g))
+                for pair in range(2):
+                    bank = take_bank("w")
+                    for b in range(2):
+                        for half in range(2):
+                            nc.tensor.transpose(
+                                bank[:, blk(2 * b + half)],
+                                words[:, 2 * pair + b, 256 * g + half : 256 * (g + 1) : 2],
+                                ident[:],
+                            )
+                    nc.scalar.copy(
+                        out=dst[:, 1024 * pair : 1024 * (pair + 1)].bitcast(F32).rearrange("p (b r u) -> p b r u", b=2, u=2),
+                        in_=bank[:].rearrange("p (b u r) -> p b r u", b=2, u=2),
+                    )
+                    give_bank("w")
+
+        def quantize_w(u):
+            n, k = divmod(u, GATES)
+            for g in range(HALVES):
+                w_q[k, g, n] = quantize(grouped["w", u, g], E4M3, "w", 16)
+
+        def turn_dzf(g, engines):
+            dst = new_grouped(("dzf", g))
+            for half in range(2):
+                bank = take_bank("dzf")
+                for j in range(PACK):
+                    words = dz_t[ORDER.index((j, g)), "f"].bitcast(F32)
+                    nc.tensor.transpose(bank[:, blk(j)], words[:, half : 256 : 2], ident[:])
+                engines[half](
+                    out=dst[:, 1024 * half : 1024 * (half + 1)].rearrange("p (c j) -> p c j", j=PACK),
+                    in_=bank[:].bitcast(BF16).rearrange("p (j c) -> p c j", j=PACK),
+                )
+                give_bank("dzf")
+
+        def quantize_dzf(g):
+            dzf_q[g] = quantize(grouped["dzf", g], E5M2, "dzf", 2)
+
+        def mx(acc, lhs, lhs_cols, lhs_fmt, rhs, rhs_fmt, start, stop):
+            nc.tensor.matmul_mx(
+                out=acc[:], lhsT=lhs[0][:, lhs_cols].bitcast(lhs_fmt), lhsT_scale=lhs[1][:, lhs_cols],
+                rhs=rhs[0][:].bitcast(rhs_fmt), rhs_scale=rhs[1][:], start=start, stop=stop,
+            )
+
+        def dx_passes(j, n, g, slots=range(GATES)):
+            for slot in slots:
+                first, final = g == 0 and slot == 0, g == HALVES - 1 and slot == GATES - 1
+                if first:
+                    accs[j, n] = take_bank(("dx", j, n))
+                mx(accs[j, n], dz_q[j, g], blk(slot), E5M2, w_q[(0, 3, 1, 2)[slot], g, n], E4M3, first, final)
+
+        def dx_group(j, n):
+            dx_passes(j, n, 0)
+            dx_passes(j, n, 1)
+
+        def dx_out(j, n, copy):
+            res = sb.tile([P, K_PASS], F32, name="res", bufs=8)
+            copy(out=res[:], in_=accs[j, n][:])
+            give_bank(("dx", j, n))
+            nc.sync.dma_start(out=out0_v[:, j, cols(n)], in_=res[:])
+
+        def dw_block(g, ib, copy):
+            acc = take_bank("dw")
+            mx(acc, x_q[ib // PACK], blk(ib % PACK), E4M3, dzf_q[g], E5M2, True, True)
+            res = sb.tile([P, K_PASS], F32, name="res", bufs=8)
+            copy(
+                out=res[:].rearrange("p (w u e) -> p w u e", u=2, e=2),
+                in_=acc[:].rearrange("p (u w e) -> p w u e", u=2, e=2),
+            )
+            give_bank("dw")
+            nc.sync.dma_start(out=out_1[blk(ib), cols(g)], in_=res[:])
+
+        on_act, on_dve = nc.scalar.copy, nc.vector.tensor_copy
+
+        load_x(0)
+        load_gates(0)
+        load_gates(1)
+        load_w(0)
+        load_gates(2)
+        load_w(1)
+        interleave_x(0, on_dve)
+        activations(0)
+        quantize_x(0)
+        load_w(2)
+        products(0)
+        transpose_cell(0)
+        activations(1)
+        load_gates(3)
+        cell_tanh(0)
+        factor_f(0)
+        factor_io(0)
+        factor_c(0)
+        transpose_factors(0, ("go", "o", "f", "i"))
+
+        def w_unit(u):
+            turn_w(u)
+            if u + 3 < 8:
+                load_w(u + 3)
+
+        units = ((0, 1), (2, 3, 4), (5, 6, 7))
+        for s in range(TILES - 2):
+            mine = units[s] if s < len(units) else ()
+            products(s + 1)
+            if 0 < s <= len(units):
+                quantize_w(units[s - 1][-1])
+            if mine:
+                w_unit(mine[0])
+            elif s < 5:
+                dx_group(s - 3, 0)
+            else:
+                dx_passes(2, 0, 0)
+            grad_cell(s)
+            transpose_factors(s, ("cc",))
+            grad_gate(s, "o")
+            activations(s + 2)
+            if s + 4 < TILES:
+                load_gates(s + 4)
+            transpose_cell(s + 1)
+            cell_tanh(s + 1)
+            for key in ("f", "i", "cc"):
+                grad_gate(s, key)
+            for u in mine[1:]:
+                w_unit(u)
+            if s == 2:
+                load_x(1)
+            if s in (3, 4):
+                dx_out(s - 3, 0, on_act)
+                dx_group(s - 3, 1)
+                dx_out(s - 3, 1, on_act)
+            if s == 3:
+                interleave_x(1, on_act)
+            if s == 5:
+                dx_passes(2, 1, 0)
+                turn_dzf(0, (on_act, on_act))
+            if len(mine) > 2:
+                quantize_w(mine[0])
+            factor_f(s + 1)
+            factor_io(s + 1)
+            factor_c(s + 1)
+            transpose_factors(s + 1, ("go", "o", "f", "i"))
+            for key in ("f", "oi", "cc"):
+                quantize_dz(s, key)
+            if mine:
+                quantize_w(mine[-2])
+            if s == 4:
+                quantize_x(1)
+
+        s, last = TILES - 2, TILES - 1
+        products(last)
+        transpose_cell(last)
+        cell_tanh(last)
+        grad_cell(s)
+        transpose_factors(s, ("cc",))
+        factor_f(last)
+        grad_gate(s, "f")
+        quantize_dzf(0)
+        transpose_factors(last, ("go", "f"))
+        grad_gate(s, "o")
+        grad_cell(last)
+        for ib in range(0, 4):
+            dw_block(0, ib, on_act)
+        grad_gate(s, "i")
+        grad_gate(last, "f")
+        turn_dzf(1, (on_act, on_act))
+        grad_gate(s, "cc")
+        factor_io(last)
+        factor_c(last)
+        for ib in range(4, 8):
+            dw_block(0, ib, on_act)
+        transpose_factors(last, ("o", "i", "cc"))
+        for key in ("f", "oi", "cc"):
+            quantize_dz(s, key)
+        quantize_dz(last, "f")
+        dx_passes(2, 0, 1)
+        dx_passes(2, 1, 1)
+        quantize_dzf(1)
+        grad_gate(last, "o")
+        dx_out(2, 0, on_act)
+        dx_out(2, 1, on_act)
+        grad_gate(last, "i")
+        quantize_dz(last, "o")
+        for ib in range(0, 4):
+            dw_block(1, ib, on_act)
+        grad_gate(last, "cc")
+        quantize_dz(last, "i")
+        quantize_dz(last, "cc")
+        dx_passes(3, 0, 0)
+        dx_passes(3, 1, 0)
+        for ib in range(4, 8):
+            dw_block(1, ib, on_dve)
+        dx_passes(3, 0, 1)
+        dx_passes(3, 1, 1)
+        dx_out(3, 0, on_act)
+        dx_out(3, 1, on_dve)

@@ -44,9 +44,9 @@ def tile_lstmcell_v_kernel(
         ident = sb.tile([P, P], F32, name="ident")
         make_identity(nc, ident[:])
 
-        raw_gates, raw_cp, raw_g, raw_w, raw_x = {}, {}, {}, {}, {}
-        sig, ct, ct2, prod, neg_p, ndc, ntc, tc2 = {}, {}, {}, {}, {}, {}, {}, {}
-        banks, dz_t, dz_q, w_q, x_q, dzf_q, grouped, accs = {}, {}, {}, {}, {}, {}, {}, {}
+        raw_gates, raw_cg, raw_w, raw_x = {}, {}, {}, {}
+        work, ct, neg_p, ndc, ntc, tc2 = {}, {}, {}, {}, {}, {}
+        banks, dz_t, dz_q, w_q, x_q, dzf_q, grouped, accs, staged = {}, {}, {}, {}, {}, {}, {}, {}, {}
 
         def cols(g):
             return slice(g * K_PASS, (g + 1) * K_PASS)
@@ -56,46 +56,47 @@ def tile_lstmcell_v_kernel(
 
         def load_gates(s):
             j, g = ORDER[s]
-            raw_gates[s] = []
-            for half in range(2):
-                t = sb.tile([P, 2 * K_PASS], F32, name="raw_gates", bufs=6)
-                raw_gates[s].append(t)
-                nc.sync.dma_start(
-                    out=t[:].rearrange("p (k h) -> p k h", k=2), in_=gates_v[:, j, 2 * half : 2 * half + 2, cols(g)]
-                )
+            raw_gates[s] = sb.tile([P, GATES * K_PASS], F32, name="raw_gates", bufs=3)
+            slots = raw_gates[s][:].rearrange("p (k h) -> p k h", k=GATES)
+            if g == 0:
+                raw_cg[j] = sb.tile([P, 2 * H], BF16, name="raw_cg", bufs=3)
+            for first, saved in enumerate((cprev_v, grad_v)):
+                nc.sync.dma_start(out=slots[:, 1 - first :: 2, :], in_=gates_v[:, j, first::2, cols(g)])
                 if g == 0:
-                    name, src, dst = (("raw_cp", cprev_v, raw_cp), ("raw_g", grad_v, raw_g))[half]
-                    dst[j] = sb.tile([P, H], BF16, name=name, bufs=3)
-                    nc.sync.dma_start(out=dst[j][:], in_=src[:, j, :])
+                    nc.sync.dma_start(out=raw_cg[j][:, first * H : (first + 1) * H], in_=saved[:, j, :])
 
         def load_w(u):
             n, k = divmod(u, GATES)
             raw_w[u] = sb.tile([P, PACK, H], BF16, name="raw_w", bufs=3)
-            nc.sync.dma_start(out=raw_w[u][:], in_=weights[k][cols(n), :].rearrange("(b p) h -> p b h", p=P))
+            nc.sync.dma_start(out=raw_w[u][:], in_=weights[k][cols(n), :].rearrange("(p b) h -> p b h", b=PACK))
 
         def load_x(n):
             raw_x[n] = sb.tile([P, PACK, K_PASS], BF16, name="raw_x", bufs=1)
             nc.sync.dma_start(out=raw_x[n][:], in_=x_v[:, :, cols(n)])
 
         def new_grouped(key):
-            grouped[key] = sb.tile([P, PACK * K_PASS], BF16, name="grouped", bufs=6, align_bytes=64)
+            grouped[key] = sb.tile([P, HALVES * PACK * K_PASS], BF16, name="grouped", bufs=3, align_bytes=64)
             return grouped[key]
 
-        def quantize(src, fmt, name, bufs):
-            codes = sb.tile([P, K_PASS], U32, name=name + "_codes", bufs=bufs, align_bytes=64)
-            scales = sb.tile([P, K_PASS], U8, name=name + "_scales", bufs=bufs, align_bytes=64)
-            nc.vector.quantize_mx(out=codes[:].bitcast(fmt), scales=scales[:], in_=src[:])
+        def quantize(src, words, fmt, name, bufs):
+            codes = sb.tile([P, words], U32, name=name + "_codes", bufs=bufs, align_bytes=64)
+            scales = sb.tile([P, words], U8, name=name + "_scales", bufs=bufs, align_bytes=64)
+            nc.vector.quantize_mx(out=codes[:].bitcast(fmt), scales=scales[:], in_=src[:, 0 : PACK * words])
             return codes, scales
 
-        def interleave_x(n, copy):
-            dst = new_grouped(("x", n))
+        def interleave_x(n, copy, part=0, parts=1):
+            if part == 0:
+                grouped["x", n] = sb.tile([P, PACK * K_PASS], BF16, name="grouped_x", bufs=1, align_bytes=64)
+            width = K_PASS // parts
             copy(
-                out=dst[:].rearrange("p (c i t) -> p c t i", i=4, t=PACK),
-                in_=raw_x[n][:].rearrange("p t (c i) -> p c t i", i=4),
+                out=grouped["x", n][:, PACK * width * part : PACK * width * (part + 1)].rearrange(
+                    "p (c i t) -> p c t i", i=4, t=PACK
+                ),
+                in_=raw_x[n][:, :, width * part : width * (part + 1)].rearrange("p t (c i) -> p c t i", i=4),
             )
 
         def quantize_x(n):
-            x_q[n] = quantize(grouped[("x", n)], E4M3, "x", 2)
+            x_q[n] = quantize(grouped["x", n], K_PASS, E4M3, "x", 2)
 
         def sorted_in(ap):
             return ap.rearrange("p (a i t) -> p a t i", i=2, t=PACK)
@@ -103,41 +104,45 @@ def tile_lstmcell_v_kernel(
         def sorted_out(ap):
             return ap.rearrange("p t (a i) -> p a t i", i=2)
 
+        def slot(s, first, count=1):
+            return work[s][:, :, first * P : (first + count) * P]
+
         def activations(s):
-            fi, co = raw_gates[s]
-            sig[s] = sb.tile([P, PACK, 3 * P], F32, name="sig", bufs=2)
+            work[s] = sb.tile([P, PACK, 7 * P], F32, name="work", bufs=2)
             ct[s] = sb.tile([P, PACK, P], F32, name="ct", bufs=2)
-            ct2[s] = sb.tile([P, PACK, P], F32, name="ct2", bufs=2)
-            nc.scalar.activation(out=sorted_out(sig[s][:, :, 0 : 2 * P]), in_=sorted_in(fi[:]), func=ACT.Sigmoid)
-            nc.scalar.activation(out=sorted_out(ct[s][:]), in_=sorted_in(co[:, 0:K_PASS]), func=ACT.Tanh)
-            nc.scalar.activation(out=sorted_out(sig[s][:, :, blk(2)]), in_=sorted_in(co[:, K_PASS:]), func=ACT.Sigmoid)
-            nc.scalar.activation(out=ct2[s][:], in_=ct[s][:], func=ACT.Square)
+            raw = raw_gates[s]
+
+            def sigmoids(first, count):
+                nc.scalar.activation(
+                    out=sorted_out(slot(s, 3 + first, count)),
+                    in_=sorted_in(raw[:, first * K_PASS : (first + count) * K_PASS]), func=ACT.Sigmoid,
+                )
+
+            sigmoids(*((1, 1) if s == 0 else (0, 3)))
+            nc.scalar.activation(out=sorted_out(ct[s][:]), in_=sorted_in(raw[:, cols(3)]), func=ACT.Tanh)
+            if s == 0:
+                sigmoids(0, 1)
+                sigmoids(2, 1)
+            nc.scalar.activation(out=slot(s, 6), in_=ct[s][:], func=ACT.Square)
 
         def products(s):
-            prod[s] = sb.tile([P, PACK, 3 * P], F32, name="prod", bufs=2)
             j, g = ORDER[s]
-            cp = raw_cp[j][:, cols(g)].rearrange("p (m t) -> p t m", t=PACK)
-            gr = raw_g[j][:, cols(g)].rearrange("p (m t) -> p t m", t=PACK)
-            nc.vector.tensor_tensor(out=prod[s][:, :, blk(0)], in0=sig[s][:, :, blk(0)], in1=cp, op=ALU.mult)
-            nc.vector.tensor_tensor(out=prod[s][:, :, blk(1)], in0=sig[s][:, :, blk(1)], in1=ct[s][:], op=ALU.mult)
-            nc.vector.tensor_tensor(out=prod[s][:, :, blk(2)], in0=sig[s][:, :, blk(2)], in1=gr, op=ALU.mult)
+            saved = raw_cg[j][:].rearrange("p (k h) -> p k h", k=2)[:, :, cols(g)]
+            nc.vector.tensor_tensor(out=slot(s, 0), in0=slot(s, 3), in1=ct[s][:], op=ALU.mult)
+            nc.vector.tensor_tensor(
+                out=slot(s, 1, 2).rearrange("p t (k m) -> p k t m", k=2),
+                in0=slot(s, 4, 2).rearrange("p t (k m) -> p k t m", k=2),
+                in1=saved.rearrange("p k (m t) -> p k t m", t=PACK),
+                op=ALU.mult,
+            )
 
-        def factor(s, key, out, in0, in1):
-            neg_p[s, key] = out
-            nc.vector.scalar_tensor_tensor(out=out, in0=in0, scalar=1.0, in1=in1, op0=ALU.subtract, op1=ALU.mult)
-
-        def factor_f(s):
-            t = sb.tile([P, PACK, P], F32, name="neg_pf", bufs=1)
-            factor(s, "f", t[:], sig[s][:, :, blk(0)], prod[s][:, :, blk(0)])
-
-        def factor_io(s):
-            t = sb.tile([P, PACK, 2 * P], F32, name="neg_pio", bufs=1)
-            factor(s, "io", t[:], sig[s][:, :, P:], prod[s][:, :, P:])
-            neg_p[s, "i"], neg_p[s, "o"] = t[:, :, blk(0)], t[:, :, blk(1)]
-
-        def factor_c(s):
-            t = sb.tile([P, PACK, P], F32, name="neg_pc", bufs=1)
-            factor(s, "cc", t[:], ct2[s][:], sig[s][:, :, blk(1)])
+        def factors(s, first=0, count=GATES):
+            if first == 0:
+                neg_p[s] = sb.tile([P, PACK, GATES * P], F32, name="neg_p", bufs=1)
+            nc.vector.scalar_tensor_tensor(
+                out=neg_p[s][:, :, first * P : (first + count) * P], in0=slot(s, 3 + first, count), scalar=1.0,
+                in1=slot(s, first, count), op0=ALU.subtract, op1=ALU.mult,
+            )
 
         free_banks = list(range(8))
         bank_of = {}
@@ -155,13 +160,13 @@ def tile_lstmcell_v_kernel(
             for t in range(PACK):
                 for term in range(2):
                     nc.tensor.matmul(
-                        out=bank[:, blk(t)], lhsT=prod[s][:, t, blk(term)], rhs=ident[:],
+                        out=bank[:, blk(t)], lhsT=work[s][:, t, blk(term)], rhs=ident[:],
                         is_transpose=True, start=(term == 0), stop=(term == 1),
                     )
 
         def transpose_factors(s, keys):
             for key in keys:
-                src = prod[s][:, :, blk(2)] if key == "go" else neg_p[s, key]
+                src = slot(s, 2) if key == "go" else neg_p[s][:, :, blk(("i", "f", "o", "cc").index(key))]
                 bank = take_bank((s, key))
                 for t in range(PACK):
                     nc.tensor.transpose(bank[:, blk(t)], src[:, t, :], ident[:])
@@ -184,31 +189,29 @@ def tile_lstmcell_v_kernel(
             give_bank((s, "go"))
 
         def grad_gate(s, key):
-            if key == "f":
-                dz_t[s, "f"] = sb.tile([P, K_PASS], BF16, name="dz_f", bufs=TILES, align_bytes=64)[:]
-            if key == "o":
-                t = sb.tile([P, 3 * K_PASS], BF16, name="dz_oic", bufs=2, align_bytes=64)
-                dz_t[s, "o"], dz_t[s, "i"], dz_t[s, "cc"] = t[:, cols(0)], t[:, cols(1)], t[:, cols(2)]
-                dz_t[s, "oi"] = t[:, 0 : 2 * K_PASS]
+            pair, place = divmod(("f", "i", "o", "cc").index(key), 2)
+            if (s, pair) not in dz_t:
+                name, bufs = (("dz_fi", TILES), ("dz_oc", 2))[pair]
+                dz_t[s, pair] = sb.tile([P, 2 * K_PASS], BF16, name=name, bufs=bufs, align_bytes=64)
             nc.vector.tensor_tensor(
-                out=dz_t[s, key].rearrange("p (n t) -> p n t", t=PACK),
+                out=dz_t[s, pair][:, cols(place)].rearrange("p (n t) -> p n t", t=PACK),
                 in0=(ntc if key == "o" else ndc)[s][:], in1=packed(s, key), op=ALU.mult,
             )
             give_bank((s, key))
 
-        def quantize_dz(s, key):
-            if key == "f":
-                codes = sb.tile([P, K_PASS], U32, name="dz_codes", bufs=6, align_bytes=64)
-                scales = sb.tile([P, K_PASS], U8, name="dz_scales", bufs=6, align_bytes=64)
+        def quantize_dz(s, pair):
+            if pair == 0:
+                codes = sb.tile([P, K_PASS], U32, name="dz_codes", bufs=5, align_bytes=64)
+                scales = sb.tile([P, K_PASS], U8, name="dz_scales", bufs=5, align_bytes=64)
                 dz_q[ORDER[s]] = codes, scales
             codes, scales = dz_q[ORDER[s]]
-            span = {"f": blk(0), "oi": slice(P, 3 * P), "o": blk(1), "i": blk(2), "cc": blk(3)}[key]
-            nc.vector.quantize_mx(out=codes[:, span].bitcast(E5M2), scales=scales[:, span], in_=dz_t[s, key])
+            span = slice(2 * P * pair, 2 * P * (pair + 1))
+            nc.vector.quantize_mx(out=codes[:, span].bitcast(E5M2), scales=scales[:, span], in_=dz_t[s, pair][:])
 
         def turn_w(u):
             words = raw_w[u][:].bitcast(F32)
+            dst = new_grouped(("w", u))
             for g in range(HALVES):
-                dst = new_grouped(("w", u, g))
                 for pair in range(2):
                     bank = take_bank("w")
                     for b in range(2):
@@ -219,22 +222,23 @@ def tile_lstmcell_v_kernel(
                                 ident[:],
                             )
                     nc.scalar.copy(
-                        out=dst[:, 1024 * pair : 1024 * (pair + 1)].bitcast(F32).rearrange("p (b r u) -> p b r u", b=2, u=2),
+                        out=dst[:, 1024 * (2 * g + pair) : 1024 * (2 * g + pair + 1)].bitcast(F32).rearrange("p (b r u) -> p b r u", b=2, u=2),
                         in_=bank[:].rearrange("p (b u r) -> p b r u", b=2, u=2),
                     )
                     give_bank("w")
 
         def quantize_w(u):
             n, k = divmod(u, GATES)
+            codes, scales = quantize(grouped["w", u], HALVES * K_PASS, E4M3, "w", 8)
             for g in range(HALVES):
-                w_q[k, g, n] = quantize(grouped["w", u, g], E4M3, "w", 16)
+                w_q[k, g, n] = codes[:, cols(g)], scales[:, cols(g)]
 
         def turn_dzf(g, engines):
             dst = new_grouped(("dzf", g))
             for half in range(2):
                 bank = take_bank("dzf")
                 for j in range(PACK):
-                    words = dz_t[ORDER.index((j, g)), "f"].bitcast(F32)
+                    words = dz_t[ORDER.index((j, g)), 0][:, 0:K_PASS].bitcast(F32)
                     nc.tensor.transpose(bank[:, blk(j)], words[:, half : 256 : 2], ident[:])
                 engines[half](
                     out=dst[:, 1024 * half : 1024 * (half + 1)].rearrange("p (c j) -> p c j", j=PACK),
@@ -243,7 +247,7 @@ def tile_lstmcell_v_kernel(
                 give_bank("dzf")
 
         def quantize_dzf(g):
-            dzf_q[g] = quantize(grouped["dzf", g], E5M2, "dzf", 2)
+            dzf_q[g] = quantize(grouped["dzf", g], K_PASS, E5M2, "dzf", 2)
 
         def mx(acc, lhs, lhs_cols, lhs_fmt, rhs, rhs_fmt, start, stop):
             nc.tensor.matmul_mx(
@@ -252,32 +256,37 @@ def tile_lstmcell_v_kernel(
             )
 
         def dx_passes(j, n, g, slots=range(GATES)):
-            for slot in slots:
-                first, final = g == 0 and slot == 0, g == HALVES - 1 and slot == GATES - 1
+            for place in slots:
+                first, final = g == 0 and place == 0, g == HALVES - 1 and place == GATES - 1
                 if first:
                     accs[j, n] = take_bank(("dx", j, n))
-                mx(accs[j, n], dz_q[j, g], blk(slot), E5M2, w_q[(0, 3, 1, 2)[slot], g, n], E4M3, first, final)
+                mx(accs[j, n], dz_q[j, g], blk(place), E5M2, w_q[(0, 1, 3, 2)[place], g, n], E4M3, first, final)
 
         def dx_group(j, n):
             dx_passes(j, n, 0)
             dx_passes(j, n, 1)
 
         def dx_out(j, n, copy):
-            res = sb.tile([P, K_PASS], F32, name="res", bufs=8)
-            copy(out=res[:], in_=accs[j, n][:])
+            res = sb.tile([P, K_PASS], F32, name="res", bufs=4)
+            copy(
+                out=res[:].rearrange("p (r b) -> p r b", b=PACK),
+                in_=accs[j, n][:].rearrange("p (b r) -> p r b", b=PACK),
+            )
             give_bank(("dx", j, n))
             nc.sync.dma_start(out=out0_v[:, j, cols(n)], in_=res[:])
 
         def dw_block(g, ib, copy):
             acc = take_bank("dw")
             mx(acc, x_q[ib // PACK], blk(ib % PACK), E4M3, dzf_q[g], E5M2, True, True)
-            res = sb.tile([P, K_PASS], F32, name="res", bufs=8)
+            if ib % PACK == 0:
+                staged[g, ib // PACK] = sb.tile([P, PACK * K_PASS], F32, name=("raw_w", "raw_gates")[g], bufs=3)
+            res = staged[g, ib // PACK][:, cols(ib % PACK)]
             copy(
-                out=res[:].rearrange("p (w u e) -> p w u e", u=2, e=2),
+                out=res.rearrange("p (w u e) -> p w u e", u=2, e=2),
                 in_=acc[:].rearrange("p (u w e) -> p w u e", u=2, e=2),
             )
             give_bank("dw")
-            nc.sync.dma_start(out=out_1[blk(ib), cols(g)], in_=res[:])
+            nc.sync.dma_start(out=out_1[blk(ib), cols(g)], in_=res)
 
         on_act, on_dve = nc.scalar.copy, nc.vector.tensor_copy
 
@@ -296,9 +305,7 @@ def tile_lstmcell_v_kernel(
         activations(1)
         load_gates(3)
         cell_tanh(0)
-        factor_f(0)
-        factor_io(0)
-        factor_c(0)
+        factors(0)
         transpose_factors(0, ("go", "o", "f", "i"))
 
         def w_unit(u):
@@ -306,18 +313,19 @@ def tile_lstmcell_v_kernel(
             if u + 3 < 8:
                 load_w(u + 3)
 
-        units = ((0, 1), (2, 3, 4), (5, 6, 7))
+        groups = {3: ((0, 0),), 4: ((0, 1), (1, 0)), 5: ((1, 1),)}
         for s in range(TILES - 2):
-            mine = units[s] if s < len(units) else ()
+            with_w = s < 4
+            ready = groups.get(s, ())
             products(s + 1)
-            if 0 < s <= len(units):
-                quantize_w(units[s - 1][-1])
-            if mine:
-                w_unit(mine[0])
-            elif s < 5:
-                dx_group(s - 3, 0)
+            if 0 < s <= 4:
+                quantize_w(2 * s - 1)
+            if s == 4:
+                quantize_x(1)
+            if with_w:
+                w_unit(2 * s)
             else:
-                dx_passes(2, 0, 0)
+                dx_group(*ready[0])
             grad_cell(s)
             transpose_factors(s, ("cc",))
             grad_gate(s, "o")
@@ -325,79 +333,77 @@ def tile_lstmcell_v_kernel(
             if s + 4 < TILES:
                 load_gates(s + 4)
             transpose_cell(s + 1)
-            cell_tanh(s + 1)
             for key in ("f", "i", "cc"):
                 grad_gate(s, key)
-            for u in mine[1:]:
-                w_unit(u)
-            if s == 2:
-                load_x(1)
-            if s in (3, 4):
-                dx_out(s - 3, 0, on_act)
-                dx_group(s - 3, 1)
-                dx_out(s - 3, 1, on_act)
-            if s == 3:
-                interleave_x(1, on_act)
             if s == 5:
-                dx_passes(2, 1, 0)
                 turn_dzf(0, (on_act, on_act))
-            if len(mine) > 2:
-                quantize_w(mine[0])
-            factor_f(s + 1)
-            factor_io(s + 1)
-            factor_c(s + 1)
+            cell_tanh(s + 1)
+            if with_w:
+                w_unit(2 * s + 1)
+            else:
+                dx_out(*ready[0], on_act)
+            if s == 1:
+                load_x(1)
+            if s in (2, 3):
+                interleave_x(1, on_act, s - 2, 2)
+            for j, n in ready[0 if with_w else 1 :]:
+                dx_group(j, n)
+                dx_out(j, n, on_act)
+            if s == 5:
+                dx_passes(2, 0, 0)
+                dx_passes(2, 1, 0)
+            factors(s + 1)
             transpose_factors(s + 1, ("go", "o", "f", "i"))
-            for key in ("f", "oi", "cc"):
-                quantize_dz(s, key)
-            if mine:
-                quantize_w(mine[-2])
-            if s == 4:
-                quantize_x(1)
+            quantize_dz(s, 0)
+            quantize_dz(s, 1)
+            if with_w:
+                quantize_w(2 * s)
 
         s, last = TILES - 2, TILES - 1
+        quantize_dzf(0)
         products(last)
+        for ib in range(0, 2):
+            dw_block(0, ib, on_act)
+        grad_cell(s)
         transpose_cell(last)
         cell_tanh(last)
-        grad_cell(s)
-        transpose_factors(s, ("cc",))
-        factor_f(last)
+        factors(last, 0, 2)
+        transpose_factors(last, ("go",))
         grad_gate(s, "f")
-        quantize_dzf(0)
-        transpose_factors(last, ("go", "f"))
+        transpose_factors(s, ("cc",))
         grad_gate(s, "o")
-        grad_cell(last)
-        for ib in range(0, 4):
-            dw_block(0, ib, on_act)
+        dw_block(0, 2, on_act)
+        transpose_factors(last, ("f",))
         grad_gate(s, "i")
+        for ib in range(3, 5):
+            dw_block(0, ib, on_act)
+        grad_cell(last)
+        grad_gate(s, "cc")
+        dw_block(0, 5, on_act)
         grad_gate(last, "f")
         turn_dzf(1, (on_act, on_act))
-        grad_gate(s, "cc")
-        factor_io(last)
-        factor_c(last)
-        for ib in range(4, 8):
-            dw_block(0, ib, on_act)
-        transpose_factors(last, ("o", "i", "cc"))
-        for key in ("f", "oi", "cc"):
-            quantize_dz(s, key)
-        quantize_dz(last, "f")
+        quantize_dz(s, 0)
+        quantize_dz(s, 1)
+        transpose_factors(last, ("i",))
+        factors(last, 2, 2)
         dx_passes(2, 0, 1)
-        dx_passes(2, 1, 1)
-        quantize_dzf(1)
-        grad_gate(last, "o")
-        dx_out(2, 0, on_act)
-        dx_out(2, 1, on_act)
         grad_gate(last, "i")
-        quantize_dz(last, "o")
-        for ib in range(0, 4):
-            dw_block(1, ib, on_act)
+        for ib in range(6, 8):
+            dw_block(0, ib, on_act)
+        transpose_factors(last, ("o", "cc"))
+        dx_out(2, 0, on_act)
+        quantize_dzf(1)
+        dx_passes(2, 1, 1)
+        grad_gate(last, "o")
+        quantize_dz(last, 0)
         grad_gate(last, "cc")
-        quantize_dz(last, "i")
-        quantize_dz(last, "cc")
-        dx_passes(3, 0, 0)
-        dx_passes(3, 1, 0)
-        for ib in range(4, 8):
-            dw_block(1, ib, on_dve)
-        dx_passes(3, 0, 1)
-        dx_passes(3, 1, 1)
+        for ib in range(0, 2):
+            dw_block(1, ib, on_act)
+        dx_out(2, 1, on_act)
+        quantize_dz(last, 1)
+        for ib in range(2, 8):
+            dw_block(1, ib, (on_dve, on_act)[ib % 2])
+        dx_group(3, 0)
         dx_out(3, 0, on_act)
+        dx_group(3, 1)
         dx_out(3, 1, on_dve)

@@ -57,13 +57,16 @@ def tile_lstmcell_v_kernel(
         def load_gates(s):
             j, g = ORDER[s]
             raw_gates[s] = sb.tile([P, GATES * K_PASS], F32, name="raw_gates", bufs=3)
-            slots = raw_gates[s][:].rearrange("p (k h) -> p k h", k=GATES)
             if g == 0:
                 raw_cg[j] = sb.tile([P, 2 * H], BF16, name="raw_cg", bufs=3)
-            for first, saved in enumerate((cprev_v, grad_v)):
-                nc.sync.dma_start(out=slots[:, 1 - first :: 2, :], in_=gates_v[:, j, first::2, cols(g)])
-                if g == 0:
-                    nc.sync.dma_start(out=raw_cg[j][:, first * H : (first + 1) * H], in_=saved[:, j, :])
+            for pair in range(2):
+                nc.sync.dma_start(
+                    out=raw_gates[s][:, 2 * pair * K_PASS : 2 * (pair + 1) * K_PASS].rearrange("p (k h) -> p k h", k=2),
+                    in_=gates_v[:, j, 2 * pair : 2 * pair + 2, cols(g)],
+                )
+            if g == 0:
+                for pair, saved in enumerate((cprev_v, grad_v)):
+                    nc.sync.dma_start(out=raw_cg[j][:, pair * H : (pair + 1) * H], in_=saved[:, j, :])
 
         def load_w(u):
             n, k = divmod(u, GATES)
@@ -102,27 +105,21 @@ def tile_lstmcell_v_kernel(
             return ap.rearrange("p (a i t) -> p a t i", i=2, t=PACK)
 
         def sorted_out(ap):
-            return ap.rearrange("p t (a i) -> p a t i", i=2)
+            return ap.rearrange("p (t a i) -> p a t i", t=PACK, i=2)
 
         def slot(s, first, count=1):
-            return work[s][:, :, first * P : (first + count) * P]
+            return work[s][:, first * K_PASS : (first + count) * K_PASS]
 
         def activations(s):
-            work[s] = sb.tile([P, PACK, 7 * P], F32, name="work", bufs=2)
-            ct[s] = sb.tile([P, PACK, P], F32, name="ct", bufs=2)
-            raw = raw_gates[s]
-
-            def sigmoids(first, count):
-                nc.scalar.activation(
-                    out=sorted_out(slot(s, 3 + first, count)),
-                    in_=sorted_in(raw[:, first * K_PASS : (first + count) * K_PASS]), func=ACT.Sigmoid,
-                )
-
-            sigmoids(*((1, 1) if s == 0 else (0, 3)))
-            nc.scalar.activation(out=sorted_out(ct[s][:]), in_=sorted_in(raw[:, cols(3)]), func=ACT.Tanh)
-            if s == 0:
-                sigmoids(0, 1)
-                sigmoids(2, 1)
+            work[s] = sb.tile([P, 7 * K_PASS], F32, name="work", bufs=2)
+            ct[s] = sb.tile([P, K_PASS], F32, name="ct", bufs=2)
+            for out, k, func in (
+                (slot(s, 3), 1, ACT.Sigmoid),
+                (slot(s, 4), 0, ACT.Sigmoid),
+                (ct[s][:], 2, ACT.Tanh),
+                (slot(s, 5), 3, ACT.Sigmoid),
+            ):
+                nc.scalar.activation(out=sorted_out(out), in_=sorted_in(raw_gates[s][:, cols(k)]), func=func)
             nc.scalar.activation(out=slot(s, 6), in_=ct[s][:], func=ACT.Square)
 
         def products(s):
@@ -130,17 +127,18 @@ def tile_lstmcell_v_kernel(
             saved = raw_cg[j][:].rearrange("p (k h) -> p k h", k=2)[:, :, cols(g)]
             nc.vector.tensor_tensor(out=slot(s, 0), in0=slot(s, 3), in1=ct[s][:], op=ALU.mult)
             nc.vector.tensor_tensor(
-                out=slot(s, 1, 2).rearrange("p t (k m) -> p k t m", k=2),
-                in0=slot(s, 4, 2).rearrange("p t (k m) -> p k t m", k=2),
+                out=slot(s, 1, 2).rearrange("p (k t m) -> p k t m", k=2, t=PACK),
+                in0=slot(s, 4, 2).rearrange("p (k t m) -> p k t m", k=2, t=PACK),
                 in1=saved.rearrange("p k (m t) -> p k t m", t=PACK),
                 op=ALU.mult,
             )
 
         def factors(s, first=0, count=GATES):
             if first == 0:
-                neg_p[s] = sb.tile([P, PACK, GATES * P], F32, name="neg_p", bufs=1)
+                name, bufs = ("raw_w", 3) if s == TILES - 1 else ("neg_p", 1)
+                neg_p[s] = sb.tile([P, GATES * K_PASS], F32, name=name, bufs=bufs)
             nc.vector.scalar_tensor_tensor(
-                out=neg_p[s][:, :, first * P : (first + count) * P], in0=slot(s, 3 + first, count), scalar=1.0,
+                out=neg_p[s][:, first * K_PASS : (first + count) * K_PASS], in0=slot(s, 3 + first, count), scalar=1.0,
                 in1=slot(s, first, count), op0=ALU.subtract, op1=ALU.mult,
             )
 
@@ -160,23 +158,23 @@ def tile_lstmcell_v_kernel(
             for t in range(PACK):
                 for term in range(2):
                     nc.tensor.matmul(
-                        out=bank[:, blk(t)], lhsT=work[s][:, t, blk(term)], rhs=ident[:],
+                        out=bank[:, blk(t)], lhsT=slot(s, term)[:, blk(t)], rhs=ident[:],
                         is_transpose=True, start=(term == 0), stop=(term == 1),
                     )
 
         def transpose_factors(s, keys):
             for key in keys:
-                src = slot(s, 2) if key == "go" else neg_p[s][:, :, blk(("i", "f", "o", "cc").index(key))]
+                src = slot(s, 2) if key == "go" else neg_p[s][:, cols(("i", "f", "o", "cc").index(key))]
                 bank = take_bank((s, key))
                 for t in range(PACK):
-                    nc.tensor.transpose(bank[:, blk(t)], src[:, t, :], ident[:])
+                    nc.tensor.transpose(bank[:, blk(t)], src[:, blk(t)], ident[:])
 
         def packed(s, key):
             return banks[s, key][:].rearrange("p (t n) -> p n t", t=PACK)
 
         def cell_tanh(s):
             ntc[s] = sb.tile([P, P, PACK], F32, name="ntc", bufs=2)
-            tc2[s] = sb.tile([P, P, PACK], F32, name="tc2", bufs=1)
+            tc2[s] = sb.tile([P, P, PACK], F32, name="tc2", bufs=2)
             nc.scalar.activation(out=ntc[s][:], in_=packed(s, "c"), func=ACT.Tanh, scale=-1.0)
             give_bank((s, "c"))
             nc.scalar.activation(out=tc2[s][:], in_=ntc[s][:], func=ACT.Square)
@@ -306,28 +304,25 @@ def tile_lstmcell_v_kernel(
         load_gates(3)
         cell_tanh(0)
         factors(0)
-        transpose_factors(0, ("go", "o", "f", "i"))
+        transpose_factors(0, ("go", "o", "f", "i", "cc"))
 
         def w_unit(u):
             turn_w(u)
             if u + 3 < 8:
                 load_w(u + 3)
 
-        groups = {3: ((0, 0),), 4: ((0, 1), (1, 0)), 5: ((1, 1),)}
-        for s in range(TILES - 2):
+        def dx_whole(j, n):
+            dx_group(j, n)
+            dx_out(j, n, on_act)
+
+        for s in range(TILES - 3):
             with_w = s < 4
-            ready = groups.get(s, ())
             products(s + 1)
-            if 0 < s <= 4:
-                quantize_w(2 * s - 1)
-            if s == 4:
-                quantize_x(1)
             if with_w:
                 w_unit(2 * s)
             else:
-                dx_group(*ready[0])
+                dx_group(1, 0)
             grad_cell(s)
-            transpose_factors(s, ("cc",))
             grad_gate(s, "o")
             activations(s + 2)
             if s + 4 < TILES:
@@ -335,75 +330,96 @@ def tile_lstmcell_v_kernel(
             transpose_cell(s + 1)
             for key in ("f", "i", "cc"):
                 grad_gate(s, key)
-            if s == 5:
-                turn_dzf(0, (on_act, on_act))
+            if 0 < s <= 4:
+                quantize_w(2 * s - 1)
             cell_tanh(s + 1)
             if with_w:
                 w_unit(2 * s + 1)
-            else:
-                dx_out(*ready[0], on_act)
             if s == 1:
                 load_x(1)
-            if s in (2, 3):
-                interleave_x(1, on_act, s - 2, 2)
-            for j, n in ready[0 if with_w else 1 :]:
-                dx_group(j, n)
-                dx_out(j, n, on_act)
-            if s == 5:
-                dx_passes(2, 0, 0)
-                dx_passes(2, 1, 0)
+            if s in (3, 4):
+                interleave_x(1, on_act, s - 3, 2)
+            if s == 3:
+                dx_whole(0, 0)
+            if s == 4:
+                dx_out(1, 0, on_act)
+                dx_whole(0, 1)
             factors(s + 1)
-            transpose_factors(s + 1, ("go", "o", "f", "i"))
+            transpose_factors(s + 1, ("go", "o", "f", "i", "cc"))
             quantize_dz(s, 0)
             quantize_dz(s, 1)
             if with_w:
                 quantize_w(2 * s)
 
-        s, last = TILES - 2, TILES - 1
+        products(6)
+        activations(7)
+        dx_group(1, 1)
+        grad_cell(5)
+        grad_gate(5, "o")
+        transpose_cell(6)
+        grad_gate(5, "f")
+        cell_tanh(6)
+        dx_out(1, 1, on_act)
+        turn_dzf(0, (on_act, on_act))
+        grad_gate(5, "i")
+        grad_gate(5, "cc")
+        products(7)
+        dx_passes(2, 0, 0)
+        transpose_cell(7)
+        cell_tanh(7)
+        factors(6, 0, 2)
+        transpose_factors(6, ("go", "f"))
+        quantize_dz(5, 0)
+        quantize_dz(5, 1)
+        quantize_x(1)
+        dx_passes(2, 1, 0)
+        grad_cell(6)
+        transpose_factors(7, ("go",))
         quantize_dzf(0)
-        products(last)
+        transpose_factors(6, ("i",))
+        factors(7, 0, 2)
         for ib in range(0, 2):
             dw_block(0, ib, on_act)
-        grad_cell(s)
-        transpose_cell(last)
-        cell_tanh(last)
-        factors(last, 0, 2)
-        transpose_factors(last, ("go",))
-        grad_gate(s, "f")
-        transpose_factors(s, ("cc",))
-        grad_gate(s, "o")
-        dw_block(0, 2, on_act)
-        transpose_factors(last, ("f",))
-        grad_gate(s, "i")
-        for ib in range(3, 5):
+        grad_gate(6, "f")
+        transpose_factors(7, ("f",))
+        grad_cell(7)
+        for ib in range(2, 4):
             dw_block(0, ib, on_act)
-        grad_cell(last)
-        grad_gate(s, "cc")
-        dw_block(0, 5, on_act)
-        grad_gate(last, "f")
+        grad_gate(6, "i")
+        for ib in range(4, 6):
+            dw_block(0, ib, on_act)
+        grad_gate(7, "f")
         turn_dzf(1, (on_act, on_act))
-        quantize_dz(s, 0)
-        quantize_dz(s, 1)
-        transpose_factors(last, ("i",))
-        factors(last, 2, 2)
-        dx_passes(2, 0, 1)
-        grad_gate(last, "i")
+        factors(6, 2, 2)
+        transpose_factors(6, ("o", "cc"))
+        factors(7, 2, 2)
+        dx_passes(3, 0, 0)
+        grad_gate(6, "o")
+        transpose_factors(7, ("i",))
+        grad_gate(6, "cc")
         for ib in range(6, 8):
             dw_block(0, ib, on_act)
-        transpose_factors(last, ("o", "cc"))
-        dx_out(2, 0, on_act)
+        transpose_factors(7, ("o",))
         quantize_dzf(1)
-        dx_passes(2, 1, 1)
-        grad_gate(last, "o")
-        quantize_dz(last, 0)
-        grad_gate(last, "cc")
-        for ib in range(0, 2):
+        quantize_dz(6, 0)
+        quantize_dz(6, 1)
+        grad_gate(7, "i")
+        transpose_factors(7, ("cc",))
+        for ib in range(0, 3):
             dw_block(1, ib, on_act)
-        dx_out(2, 1, on_act)
-        quantize_dz(last, 1)
-        for ib in range(2, 8):
-            dw_block(1, ib, (on_dve, on_act)[ib % 2])
-        dx_group(3, 0)
-        dx_out(3, 0, on_act)
+        grad_gate(7, "o")
+        dx_passes(2, 0, 1)
+        quantize_dz(7, 0)
+        grad_gate(7, "cc")
+        for ib in range(3, 5):
+            dw_block(1, ib, on_act)
+        dx_passes(2, 1, 1)
+        quantize_dz(7, 1)
+        dx_out(2, 0, on_dve)
+        for ib in range(5, 8):
+            dw_block(1, ib, on_act)
+        dx_out(2, 1, on_dve)
+        dx_passes(3, 0, 1)
+        dx_out(3, 0, on_dve)
         dx_group(3, 1)
-        dx_out(3, 1, on_dve)
+        dx_out(3, 1, on_act)

@@ -124,14 +124,15 @@ def tile_lstmcell_v_kernel(
 
         def products(s):
             j, g = ORDER[s]
-            saved = raw_cg[j][:].rearrange("p (k h) -> p k h", k=2)[:, :, cols(g)]
             nc.vector.tensor_tensor(out=slot(s, 0), in0=slot(s, 3), in1=ct[s][:], op=ALU.mult)
-            nc.vector.tensor_tensor(
-                out=slot(s, 1, 2).rearrange("p (k t m) -> p k t m", k=2, t=PACK),
-                in0=slot(s, 4, 2).rearrange("p (k t m) -> p k t m", k=2, t=PACK),
-                in1=saved.rearrange("p k (m t) -> p k t m", t=PACK),
-                op=ALU.mult,
-            )
+            for k in range(2):
+                saved = raw_cg[j][:, k * H + g * K_PASS : k * H + (g + 1) * K_PASS]
+                nc.vector.tensor_tensor(
+                    out=slot(s, 1 + k).rearrange("p (t a i) -> p a t i", t=PACK, i=4),
+                    in0=slot(s, 4 + k).rearrange("p (t a i) -> p a t i", t=PACK, i=4),
+                    in1=saved.rearrange("p (a i t) -> p a t i", t=PACK, i=4),
+                    op=ALU.mult,
+                )
 
         def factors(s, first=0, count=GATES):
             if first == 0:
@@ -325,8 +326,6 @@ def tile_lstmcell_v_kernel(
             grad_cell(s)
             grad_gate(s, "o")
             activations(s + 2)
-            if s + 4 < TILES:
-                load_gates(s + 4)
             transpose_cell(s + 1)
             for key in ("f", "i", "cc"):
                 grad_gate(s, key)
@@ -335,7 +334,9 @@ def tile_lstmcell_v_kernel(
             cell_tanh(s + 1)
             if with_w:
                 w_unit(2 * s + 1)
-            if s == 1:
+            if s + 4 < TILES:
+                load_gates(s + 4)
+            if s == 2:
                 load_x(1)
             if s in (3, 4):
                 interleave_x(1, on_act, s - 3, 2)

@@ -45,7 +45,7 @@ def tile_lstmcell_v_kernel(
         make_identity(nc, ident[:])
 
         raw_gates, raw_cg, raw_w, raw_x = {}, {}, {}, {}
-        work, ct, neg_p, ndc, ntc, tc2 = {}, {}, {}, {}, {}, {}
+        work, ct, neg_p, ndc, ntc, tc2, cell = {}, {}, {}, {}, {}, {}, {}
         banks, dz_t, dz_q, w_q, x_q, dzf_q, grouped, accs, staged = {}, {}, {}, {}, {}, {}, {}, {}, {}
 
         def cols(g):
@@ -124,8 +124,9 @@ def tile_lstmcell_v_kernel(
 
         def products(s):
             j, g = ORDER[s]
-            nc.vector.tensor_tensor(out=slot(s, 0), in0=slot(s, 3), in1=ct[s][:], op=ALU.mult)
-            for k in range(2):
+            if s == 0:
+                nc.vector.tensor_tensor(out=slot(s, 0), in0=slot(s, 3), in1=ct[s][:], op=ALU.mult)
+            for k in (0, 1) if s == 0 else (1, 0):
                 saved = raw_cg[j][:, k * H + g * K_PASS : k * H + (g + 1) * K_PASS]
                 nc.vector.tensor_tensor(
                     out=slot(s, 1 + k).rearrange("p (t a i) -> p a t i", t=PACK, i=4),
@@ -133,6 +134,12 @@ def tile_lstmcell_v_kernel(
                     in1=saved.rearrange("p (a i t) -> p a t i", t=PACK, i=4),
                     op=ALU.mult,
                 )
+
+            if s > 0:
+                nc.vector.tensor_tensor(out=slot(s, 0), in0=slot(s, 3), in1=ct[s][:], op=ALU.mult)
+            if 0 < s < TILES - 1:
+                cell[s] = sb.tile([P, K_PASS], F32, name="cell", bufs=1)
+                nc.gpsimd.tensor_tensor(out=cell[s][:], in0=slot(s, 0), in1=slot(s, 1), op=ALU.add)
 
         def factors(s, first=0, count=GATES):
             if first == 0:
@@ -157,7 +164,9 @@ def tile_lstmcell_v_kernel(
         def transpose_cell(s):
             bank = take_bank((s, "c"))
             for t in range(PACK):
-                for term in range(2):
+                if s in cell:
+                    nc.tensor.transpose(bank[:, blk(t)], cell[s][:, blk(t)], ident[:])
+                for term in range(0 if s in cell else 2):
                     nc.tensor.matmul(
                         out=bank[:, blk(t)], lhsT=slot(s, term)[:, blk(t)], rhs=ident[:],
                         is_transpose=True, start=(term == 0), stop=(term == 1),

from contextlib import ExitStack

import concourse.mybir as mybir
from concourse.masks import make_identity

B, I, H = 512, 1024, 1024
FLOPS = 2 * B * 4 * H * I + 2 * I * B * H
BYTES = (B * I + 2 * B * H + 4 * I * H) * 2 + (B * 4 * H + B * I + I * H) * 4

F32 = mybir.dt.float32
BF16 = mybir.dt.bfloat16
U32 = mybir.dt.uint32
U8 = mybir.dt.uint8
E4M3 = mybir.dt.float8_e4m3fn_x4
E5M2 = mybir.dt.float8_e5m2_x4
ACT = mybir.ActivationFunctionType
ALU = mybir.AluOpType

P = 128
PACK = 4
K_PASS = P * PACK
GATES = 4
HALVES = 2
TILES = HALVES * PACK
ORDER = ((0, 0), (0, 1), (1, 0), (1, 1), (2, 0), (3, 0), (2, 1), (3, 1))


def tile_lstmcell_v_kernel(
    tc, x_t, h_prev, c_prev, W_f, W_i, W_c, W_o, U_f, U_i, U_c, U_o, b_f, b_i, b_c, b_o, gates, grad_out, out_0, out_1
):
    nc = tc.nc
    weights = (W_f, W_i, W_c, W_o)
    gates_v = gates.rearrange("(p j) (k h) -> p j k h", j=PACK, k=GATES)
    cprev_v = c_prev.rearrange("(p j) h -> p j h", j=PACK)
    grad_v = grad_out.rearrange("(p j) h -> p j h", j=PACK)
    x_v = x_t.rearrange("(p j) i -> p j i", j=PACK)
    out0_v = out_0.rearrange("(p j) i -> p j i", j=PACK)

    with ExitStack() as ctx:
        sb = ctx.enter_context(tc.tile_pool(name="sb", bufs=1))
        ps = ctx.enter_context(tc.psum_pool(name="ps", bufs=1))
        ctx.enter_context(tc.manual_schedule())

        ident = sb.tile([P, P], F32, name="ident")
        make_identity(nc, ident[:])

        raw_gates, raw_cg, raw_w, raw_x = {}, {}, {}, {}
        work, ct, neg_p, ndc, ntc, tc2, cell = {}, {}, {}, {}, {}, {}, {}
        banks, dz_t, dz_q, w_q, x_q, dzf_q, grouped, accs, staged = {}, {}, {}, {}, {}, {}, {}, {}, {}

        def cols(g):
            return slice(g * K_PASS, (g + 1) * K_PASS)

        def blk(t):
            return slice(t * P, (t + 1) * P)

        def load_gates(s):
            j, g = ORDER[s]
            raw_gates[s] = sb.tile([P, GATES * K_PASS], F32, name="raw_gates", bufs=3)
            if g == 0:
                raw_cg[j] = sb.tile([P, 2 * H], BF16, name="raw_cg", bufs=3)
            for pair in range(2):
                nc.sync.dma_start(
                    out=raw_gates[s][:, 2 * pair * K_PASS : 2 * (pair + 1) * K_PASS].rearrange("p (k h) -> p k h", k=2),
                    in_=gates_v[:, j, 2 * pair : 2 * pair + 2, cols(g)],
                )
            if g == 0:
                for pair, saved in enumerate((cprev_v, grad_v)):
                    nc.sync.dma_start(out=raw_cg[j][:, pair * H : (pair + 1) * H], in_=saved[:, j, :])

        def load_w(u):
            n, k = divmod(u, GATES)
            raw_w[u] = sb.tile([P, PACK, H], BF16, name="raw_w", bufs=3)
            nc.sync.dma_start(out=raw_w[u][:], in_=weights[k][cols(n), :].rearrange("(p b) h -> p b h", b=PACK))

        def load_x(n):
            raw_x[n] = sb.tile([P, PACK, K_PASS], BF16, name="raw_x", bufs=1)
            nc.sync.dma_start(out=raw_x[n][:], in_=x_v[:, :, cols(n)])

        def new_grouped(key):
            grouped[key] = sb.tile([P, HALVES * PACK * K_PASS], BF16, name="grouped", bufs=3, align_bytes=64)
            return grouped[key]

        def quantize(src, words, fmt, name, bufs):
            codes = sb.tile([P, words], U32, name=name + "_codes", bufs=bufs, align_bytes=64)
            scales = sb.tile([P, words], U8, name=name + "_scales", bufs=bufs, align_bytes=64)
            nc.vector.quantize_mx(out=codes[:].bitcast(fmt), scales=scales[:], in_=src[:, 0 : PACK * words])
            return codes, scales

        def interleave_x(n, copy, part=0, parts=1):
            if part == 0:
                grouped["x", n] = sb.tile([P, PACK * K_PASS], BF16, name="grouped_x", bufs=1, align_bytes=64)
            width = K_PASS // parts
            copy(
                out=grouped["x", n][:, PACK * width * part : PACK * width * (part + 1)].rearrange(
                    "p (c i t) -> p c t i", i=4, t=PACK
                ),
                in_=raw_x[n][:, :, width * part : width * (part + 1)].rearrange("p t (c i) -> p c t i", i=4),
            )

        def quantize_x(n):
            x_q[n] = quantize(grouped["x", n], K_PASS, E4M3, "x", 2)

        def sorted_in(ap):
            return ap.rearrange("p (a i t) -> p a t i", i=2, t=PACK)

        def sorted_out(ap):
            return ap.rearrange("p (t a i) -> p a t i", t=PACK, i=2)

        def slot(s, first, count=1):
            return work[s][:, first * K_PASS : (first + count) * K_PASS]

        def activations(s):
            work[s] = sb.tile([P, 7 * K_PASS], F32, name="work", bufs=2)
            ct[s] = sb.tile([P, K_PASS], F32, name="ct", bufs=2)
            for out, k, func in (
                (slot(s, 3), 1, ACT.Sigmoid),
                (slot(s, 4), 0, ACT.Sigmoid),
                (ct[s][:], 2, ACT.Tanh),
                (slot(s, 5), 3, ACT.Sigmoid),
            ):
                nc.scalar.activation(out=sorted_out(out), in_=sorted_in(raw_gates[s][:, cols(k)]), func=func)
            nc.scalar.activation(out=slot(s, 6), in_=ct[s][:], func=ACT.Square)

        def products(s):
            j, g = ORDER[s]
            if s == 0:
                nc.vector.tensor_tensor(out=slot(s, 0), in0=slot(s, 3), in1=ct[s][:], op=ALU.mult)
            for k in (0, 1) if s == 0 else (1, 0):
                saved = raw_cg[j][:, k * H + g * K_PASS : k * H + (g + 1) * K_PASS]
                nc.vector.tensor_tensor(
                    out=slot(s, 1 + k).rearrange("p (t a i) -> p a t i", t=PACK, i=4),
                    in0=slot(s, 4 + k).rearrange("p (t a i) -> p a t i", t=PACK, i=4),
                    in1=saved.rearrange("p (a i t) -> p a t i", t=PACK, i=4),
                    op=ALU.mult,
                )

            if s > 0:
                nc.vector.tensor_tensor(out=slot(s, 0), in0=slot(s, 3), in1=ct[s][:], op=ALU.mult)
            if 0 < s < TILES - 1:
                cell[s] = sb.tile([P, K_PASS], F32, name="cell", bufs=1)
                nc.gpsimd.tensor_tensor(out=cell[s][:], in0=slot(s, 0), in1=slot(s, 1), op=ALU.add)

        def factors(s, first=0, count=GATES):
            if first == 0:
                name, bufs = ("raw_w", 3) if s == TILES - 1 else ("neg_p", 1)
                neg_p[s] = sb.tile([P, GATES * K_PASS], F32, name=name, bufs=bufs)
            nc.vector.scalar_tensor_tensor(
                out=neg_p[s][:, first * K_PASS : (first + count) * K_PASS], in0=slot(s, 3 + first, count), scalar=1.0,
                in1=slot(s, first, count), op0=ALU.subtract, op1=ALU.mult,
            )

        free_banks = list(range(8))
        bank_of = {}

        def take_bank(key):
            bank_of[key] = free_banks.pop(0)
            banks[key] = ps.tile([P, K_PASS], F32, name="bank%d" % bank_of[key])
            return banks[key]

        def give_bank(key):
            free_banks.append(bank_of[key])

        def transpose_cell(s):
            bank = take_bank((s, "c"))
            for t in range(PACK):
                if s in cell:
                    nc.tensor.transpose(bank[:, blk(t)], cell[s][:, blk(t)], ident[:])
                for term in range(0 if s in cell else 2):
                    nc.tensor.matmul(
                        out=bank[:, blk(t)], lhsT=slot(s, term)[:, blk(t)], rhs=ident[:],
                        is_transpose=True, start=(term == 0), stop=(term == 1),
                    )

        def transpose_factors(s, keys):
            for key in keys:
                src = slot(s, 2) if key == "go" else neg_p[s][:, cols(("i", "f", "o", "cc").index(key))]
                bank = take_bank((s, key))
                for t in range(PACK):
                    nc.tensor.transpose(bank[:, blk(t)], src[:, blk(t)], ident[:])

        def packed(s, key):
            return banks[s, key][:].rearrange("p (t n) -> p n t", t=PACK)

        def cell_tanh(s):
            ntc[s] = sb.tile([P, P, PACK], F32, name="ntc", bufs=2)
            tc2[s] = sb.tile([P, P, PACK], F32, name="tc2", bufs=2)
            nc.scalar.activation(out=ntc[s][:], in_=packed(s, "c"), func=ACT.Tanh, scale=-1.0)
            give_bank((s, "c"))
            nc.scalar.activation(out=tc2[s][:], in_=ntc[s][:], func=ACT.Square)

        def grad_cell(s):
            ndc[s] = sb.tile([P, P, PACK], F32, name="ndc", bufs=2)
            nc.vector.scalar_tensor_tensor(
                out=ndc[s][:], in0=tc2[s][:], scalar=1.0, in1=packed(s, "go"), op0=ALU.subtract, op1=ALU.mult
            )
            give_bank((s, "go"))

        def grad_gate(s, key):
            pair, place = divmod(("f", "i", "o", "cc").index(key), 2)
            if (s, pair) not in dz_t:
                name, bufs = (("dz_fi", TILES), ("dz_oc", 2))[pair]
                dz_t[s, pair] = sb.tile([P, 2 * K_PASS], BF16, name=name, bufs=bufs, align_bytes=64)
            nc.vector.tensor_tensor(
                out=dz_t[s, pair][:, cols(place)].rearrange("p (n t) -> p n t", t=PACK),
                in0=(ntc if key == "o" else ndc)[s][:], in1=packed(s, key), op=ALU.mult,
            )
            give_bank((s, key))

        def quantize_dz(s, pair):
            if pair == 0:
                codes = sb.tile([P, K_PASS], U32, name="dz_codes", bufs=5, align_bytes=64)
                scales = sb.tile([P, K_PASS], U8, name="dz_scales", bufs=5, align_bytes=64)
                dz_q[ORDER[s]] = codes, scales
            codes, scales = dz_q[ORDER[s]]
            span = slice(2 * P * pair, 2 * P * (pair + 1))
            nc.vector.quantize_mx(out=codes[:, span].bitcast(E5M2), scales=scales[:, span], in_=dz_t[s, pair][:])

        def turn_w(u):
            words = raw_w[u][:].bitcast(F32)
            dst = new_grouped(("w", u))
            for g in range(HALVES):
                for pair in range(2):
                    bank = take_bank("w")
                    for b in range(2):
                        for half in range(2):
                            nc.tensor.transpose(
                                bank[:, blk(2 * b + half)],
                                words[:, 2 * pair + b, 256 * g + half : 256 * (g + 1) : 2],
                                ident[:],
                            )
                    nc.scalar.copy(
                        out=dst[:, 1024 * (2 * g + pair) : 1024 * (2 * g + pair + 1)].bitcast(F32).rearrange("p (b r u) -> p b r u", b=2, u=2),
                        in_=bank[:].rearrange("p (b u r) -> p b r u", b=2, u=2),
                    )
                    give_bank("w")

        def quantize_w(u):
            n, k = divmod(u, GATES)
            codes, scales = quantize(grouped["w", u], HALVES * K_PASS, E4M3, "w", 8)
            for g in range(HALVES):
                w_q[k, g, n] = codes[:, cols(g)], scales[:, cols(g)]

        def turn_dzf(g, engines):
            dst = new_grouped(("dzf", g))
            for half in range(2):
                bank = take_bank("dzf")
                for j in range(PACK):
                    words = dz_t[ORDER.index((j, g)), 0][:, 0:K_PASS].bitcast(F32)
                    nc.tensor.transpose(bank[:, blk(j)], words[:, half : 256 : 2], ident[:])
                engines[half](
                    out=dst[:, 1024 * half : 1024 * (half + 1)].rearrange("p (c j) -> p c j", j=PACK),
                    in_=bank[:].bitcast(BF16).rearrange("p (j c) -> p c j", j=PACK),
                )
                give_bank("dzf")

        def quantize_dzf(g):
            dzf_q[g] = quantize(grouped["dzf", g], K_PASS, E5M2, "dzf", 2)

        def mx(acc, lhs, lhs_cols, lhs_fmt, rhs, rhs_fmt, start, stop):
            nc.tensor.matmul_mx(
                out=acc[:], lhsT=lhs[0][:, lhs_cols].bitcast(lhs_fmt), lhsT_scale=lhs[1][:, lhs_cols],
                rhs=rhs[0][:].bitcast(rhs_fmt), rhs_scale=rhs[1][:], start=start, stop=stop,
            )

        def dx_passes(j, n, g, slots=range(GATES)):
            for place in slots:
                first, final = g == 0 and place == 0, g == HALVES - 1 and place == GATES - 1
                if first:
                    accs[j, n] = take_bank(("dx", j, n))
                mx(accs[j, n], dz_q[j, g], blk(place), E5M2, w_q[(0, 1, 3, 2)[place], g, n], E4M3, first, final)

        def dx_group(j, n):
            dx_passes(j, n, 0)
            dx_passes(j, n, 1)

        def dx_out(j, n, copy):
            res = sb.tile([P, K_PASS], F32, name="res", bufs=4)
            copy(
                out=res[:].rearrange("p (r b) -> p r b", b=PACK),
                in_=accs[j, n][:].rearrange("p (b r) -> p r b", b=PACK),
            )
            give_bank(("dx", j, n))
            nc.sync.dma_start(out=out0_v[:, j, cols(n)], in_=res[:])

        def dw_block(g, ib, copy):
            acc = take_bank("dw")
            mx(acc, x_q[ib // PACK], blk(ib % PACK), E4M3, dzf_q[g], E5M2, True, True)
            if ib % PACK == 0:
                staged[g, ib // PACK] = sb.tile([P, PACK * K_PASS], F32, name=("raw_w", "raw_gates")[g], bufs=3)
            res = staged[g, ib // PACK][:, cols(ib % PACK)]
            copy(
                out=res.rearrange("p (w u e) -> p w u e", u=2, e=2),
                in_=acc[:].rearrange("p (u w e) -> p w u e", u=2, e=2),
            )
            give_bank("dw")
            nc.sync.dma_start(out=out_1[blk(ib), cols(g)], in_=res)

        on_act, on_dve = nc.scalar.copy, nc.vector.tensor_copy

        load_x(0)
        load_gates(0)
        load_gates(1)
        load_w(0)
        load_gates(2)
        load_w(1)
        interleave_x(0, on_dve)
        activations(0)
        quantize_x(0)
        load_w(2)
        products(0)
        transpose_cell(0)
        activations(1)
        load_gates(3)
        cell_tanh(0)
        factors(0)
        transpose_factors(0, ("go", "o", "f", "i", "cc"))

        def w_unit(u):
            turn_w(u)
            if u + 3 < 8:
                load_w(u + 3)

        def dx_whole(j, n):
            dx_group(j, n)
            dx_out(j, n, on_act)

        for s in range(TILES - 3):
            with_w = s < 4
            products(s + 1)
            if with_w:
                w_unit(2 * s)
            else:
                dx_group(1, 0)
            grad_cell(s)
            grad_gate(s, "o")
            activations(s + 2)
            transpose_cell(s + 1)
            for key in ("f", "i", "cc"):
                grad_gate(s, key)
            if 0 < s <= 4:
                quantize_w(2 * s - 1)
            cell_tanh(s + 1)
            if with_w:
                w_unit(2 * s + 1)
            if s + 4 < TILES:
                load_gates(s + 4)
            if s == 2:
                load_x(1)
            if s in (3, 4):
                interleave_x(1, on_act, s - 3, 2)
            if s == 3:
                dx_whole(0, 0)
            if s == 4:
                dx_out(1, 0, on_act)
                dx_whole(0, 1)
            factors(s + 1)
            transpose_factors(s + 1, ("go", "o", "f", "i", "cc"))
            quantize_dz(s, 0)
            quantize_dz(s, 1)
            if with_w:
                quantize_w(2 * s)

        products(6)
        activations(7)
        dx_group(1, 1)
        grad_cell(5)
        grad_gate(5, "o")
        transpose_cell(6)
        grad_gate(5, "f")
        cell_tanh(6)
        dx_out(1, 1, on_act)
        turn_dzf(0, (on_act, on_act))
        grad_gate(5, "i")
        grad_gate(5, "cc")
        products(7)
        dx_passes(2, 0, 0)
        transpose_cell(7)
        cell_tanh(7)
        factors(6, 0, 2)
        transpose_factors(6, ("go", "f"))
        quantize_dz(5, 0)
        quantize_dz(5, 1)
        quantize_x(1)
        dx_passes(2, 1, 0)
        grad_cell(6)
        transpose_factors(7, ("go",))
        quantize_dzf(0)
        transpose_factors(6, ("i",))
        factors(7, 0, 2)
        for ib in range(0, 2):
            dw_block(0, ib, on_act)
        grad_gate(6, "f")
        transpose_factors(7, ("f",))
        grad_cell(7)
        for ib in range(2, 4):
            dw_block(0, ib, on_act)
        grad_gate(6, "i")
        for ib in range(4, 6):
            dw_block(0, ib, on_act)
        grad_gate(7, "f")
        turn_dzf(1, (on_act, on_act))
        factors(6, 2, 2)
        transpose_factors(6, ("o", "cc"))
        factors(7, 2, 2)
        dx_passes(3, 0, 0)
        grad_gate(6, "o")
        transpose_factors(7, ("i",))
        grad_gate(6, "cc")
        for ib in range(6, 8):
            dw_block(0, ib, on_act)
        transpose_factors(7, ("o",))
        quantize_dzf(1)
        quantize_dz(6, 0)
        quantize_dz(6, 1)
        grad_gate(7, "i")
        transpose_factors(7, ("cc",))
        for ib in range(0, 3):
            dw_block(1, ib, on_act)
        grad_gate(7, "o")
        dx_passes(2, 0, 1)
        quantize_dz(7, 0)
        grad_gate(7, "cc")
        for ib in range(3, 5):
            dw_block(1, ib, on_act)
        dx_passes(2, 1, 1)
        quantize_dz(7, 1)
        dx_out(2, 0, on_dve)
        for ib in range(5, 8):
            dw_block(1, ib, on_act)
        dx_out(2, 1, on_dve)
        dx_passes(3, 0, 1)
        dx_out(3, 0, on_dve)
        dx_group(3, 1)
        dx_out(3, 1, on_act)
